import numpy as np
import ml_dtypes


BF16 = ml_dtypes.bfloat16


def bf(x):
    return np.asarray(x, np.float32).astype(BF16)


def f64(x):
    return np.asarray(x).astype(np.float64)


E2M1 = np.array([0.0, 0.5, 1.0, 1.5, 2.0, 3.0, 4.0, 6.0, -0.0, -0.5, -1.0, -1.5, -2.0, -3.0, -4.0, -6.0])


def pack_weight(w, fmt):
    k, n = w.shape
    w = f64(bf(w)).reshape(k // 32, 32, n)
    amax = np.abs(w).max(1)
    if fmt == "e4m3":
        byte = np.frexp(amax)[1] - 1 + 127 - 7
    else:
        mant, ex = np.frexp(amax / 6.0)
        byte = np.where(mant > 0.5, ex, ex - 1) + 127
    byte = np.clip(np.where(amax > 0, byte, 1), 1, 254)
    scaled = (w * np.exp2(127.0 - byte)[:, None, :]).reshape(k, n).astype(np.float32)
    by_word = np.ascontiguousarray(scaled.reshape(k // 512, 128, 4, n).transpose(0, 1, 3, 2))
    if fmt == "e4m3":
        words = by_word.astype(ml_dtypes.float8_e4m3fn).view(np.uint8)
    else:
        c = by_word.astype(ml_dtypes.float4_e2m1fn).view(np.uint8) & 0xF
        words = c[..., 0::2] | (c[..., 1::2] << 4)
    return np.ascontiguousarray(words), np.ascontiguousarray(byte.astype(np.uint8).reshape(k // 512, 16, n))


def unpack_weight(words, scales, fmt):
    g, p, n, _ = words.shape
    if fmt == "e4m3":
        vals = np.ascontiguousarray(words).view(ml_dtypes.float8_e4m3fn).astype(np.float64)
    else:
        nib = np.empty((g, p, n, 4), np.uint8)
        nib[..., 0::2] = words & 0xF
        nib[..., 1::2] = words >> 4
        vals = E2M1[nib]
    vals = vals * np.repeat(np.exp2(scales.astype(np.float64) - 127.0), 8, axis=1)[..., None]
    return vals.transpose(0, 1, 3, 2).reshape(g * 512, n)

def pack4(w):
    words, scales = pack_weight(w, "e2m1")
    return words.reshape(words.shape[0], 128, -1), scales


def unpack4(words, scales):
    return unpack_weight(words.reshape(words.shape[0], 128, -1, 2), scales, "e2m1")


def kspread(k):
    return np.exp2(np.repeat(np.random.randint(-6, 7, k // 32), 32).astype(np.float64))


B, T, C, NH, NKV, HS = 2, 1536, 2048, 16, 4, 128
EPS = 1e-6
ROPE_THETA = 10000.0
HALF = HS // 2
KW = NKV * HS


def rmsnorm(u, gain):
    ms = np.mean(np.square(u), axis=-1, keepdims=True)
    return u * (1.0 / np.sqrt(ms + EPS)) * gain


def rope_cos_sin():
    inv_freq = ROPE_THETA ** (-np.arange(0, HS, 2, dtype=np.float64) / HS)
    ang = np.arange(T, dtype=np.float64)[:, None] * inv_freq[None, :]
    return np.cos(ang), np.sin(ang)


def apply_rope(u, cos, sin):
    u1, u2 = u[..., :HALF], u[..., HALF:]
    c = cos[None, :, None, :]
    s = sin[None, :, None, :]
    return np.concatenate([u1 * c - u2 * s, u1 * s + u2 * c], axis=-1)


def setup_inputs():
    s = kspread(C)
    x = np.random.standard_normal((B, T, C)) * s
    x_words, x_scales = pack4(x.reshape(B * T, C).T)
    Wq_words, Wq_scales = pack4(np.random.standard_normal((C, NH * HS)) / np.sqrt(C) / s[:, None])
    Wkv_words, Wkv_scales = pack4(np.random.standard_normal((C, 2 * KW)) / np.sqrt(C) / s[:, None])
    return {
        "x_words": x_words,
        "x_scales": x_scales,
        "Wq_words": Wq_words,
        "Wq_scales": Wq_scales,
        "Wkv_words": Wkv_words,
        "Wkv_scales": Wkv_scales,
        "q_scale": bf(1.0 + 0.1 * np.random.standard_normal(HS)),
        "k_scale": bf(1.0 + 0.1 * np.random.standard_normal(HS)),
        "v1": bf(np.random.standard_normal((B, T, NKV, HS))),
        "value_lambda": bf(np.random.uniform(0.2, 0.7, (1,))),
    }


def reference(x_words, x_scales, Wq_words, Wq_scales, Wkv_words, Wkv_scales, q_scale, k_scale, v1, value_lambda):
    xq = unpack4(x_words, x_scales).T.reshape(B, T, C)
    q = (xq @ unpack4(Wq_words, Wq_scales)).reshape(B, T, NH, HS)
    kv = xq @ unpack4(Wkv_words, Wkv_scales)
    k = kv[..., :KW].reshape(B, T, NKV, HS)
    v = kv[..., KW:].reshape(B, T, NKV, HS)
    lam = f64(value_lambda).reshape(())
    v = v + (1.0 - lam) * f64(v1)
    q = rmsnorm(q, f64(q_scale))
    k = rmsnorm(k, f64(k_scale))
    cos, sin = rope_cos_sin()
    return apply_rope(q, cos, sin), apply_rope(k, cos, sin), v

@@ -1,0 +1,363 @@
+from contextlib import ExitStack
+import math
+
+import concourse.mybir as mybir
+
+F32 = mybir.dt.float32
+BF16 = mybir.dt.bfloat16
+I32 = mybir.dt.int32
+U32 = mybir.dt.uint32
+U8 = mybir.dt.uint8
+FP4 = mybir.dt.float4_e2m1fn_x4
+ALU = mybir.AluOpType
+ACT = mybir.ActivationFunctionType
+
+NB, T, C = 2, 1536, 2048
+NH, NKV, HS = 16, 4, 128
+HALF = HS // 2
+EPS = 1e-6
+THETA = 10000.0
+P = 128
+PASSES = C // 512
+NJ = T // P
+BANK = 512
+FLOPS = 2 * NB * T * C * (NH * HS + 2 * NKV * HS)
+
+JCH = ((0, 2), (2, 6), (6, 12))
+GROUPS = ((0, 1, 2), (3, 4))
+TCH = ((0, 1), (1, 12))
+LAG_SS = 1
+LAG_V = 2
+LAG_RS = 6
+N_WARM = 10
+T1_BUFS = 4
+T2_BUFS = 3
+
+
+def tile_attention_pa_kernel(
+    tc, x_words, x_scales, Wq_words, Wq_scales, Wkv_words, Wkv_scales,
+    q_scale, k_scale, v1, value_lambda, out_0, out_1, out_2,
+):
+    nc = tc.nc
+    out0f = out_0.rearrange("b t h d -> (b t) (h d)")
+    out1f = out_1.rearrange("b t h d -> (b t) (h d)")
+    out2f = out_2.rearrange("b t h d -> (b t) (h d)")
+    v1f = v1.rearrange("b t h d -> (b t) (h d)")
+
+    with ExitStack() as ctx:
+        ctx.enter_context(tc.manual_schedule())
+        keep = ctx.enter_context(tc.tile_pool(name="keep", bufs=1))
+        psum = ctx.enter_context(tc.psum_pool(name="psum", bufs=8))
+        work = ctx.enter_context(tc.tile_pool(name="work", bufs=2))
+
+        chunks = [(b, c) for c in range(len(JCH)) for b in range(NB)]
+        xc, xs, v1c = {}, {}, {}
+        for b, c in chunks:
+            nj = JCH[c][1] - JCH[c][0]
+            xc[(b, c)] = keep.tile([P, PASSES, 256 * nj], U8, name="xc%d%d" % (b, c), align_bytes=64)
+            xs[(b, c)] = keep.tile([P, PASSES, P * nj], U8, name="xs%d%d" % (b, c), align_bytes=64)
+            v1c[(b, c)] = keep.tile([P, nj, BANK], BF16, name="v1c%d%d" % (b, c))
+        wc = [keep.tile([P, PASSES, 2 * BANK], U8, name="wc%d" % w, align_bytes=64) for w in range(6)]
+        ws_a = keep.tile([P, PASSES, BANK], U8, name="ws_a", align_bytes=64)
+        ws_b = keep.tile([P, PASSES, 3 * BANK], U8, name="ws_b", align_bytes=64)
+        ws_kv = keep.tile([P, PASSES, 2 * BANK], U8, name="ws_kv", align_bytes=64)
+
+        def w_plane(w, g):
+            if w == 0:
+                return ws_a[:, g, :]
+            if w < 4:
+                return ws_b[:, g, (w - 1) * BANK : w * BANK]
+            return ws_kv[:, g, (w - 4) * BANK : (w - 3) * BANK]
+
+        ones = keep.tile([P, 8], F32, name="ones")
+        a8 = keep.tile([P, 8], F32, name="a8")
+        b8 = keep.tile([P, 8], F32, name="b8")
+        turn = keep.tile([P, HALF], F32, name="turn")
+        pos = keep.tile([P, NJ], F32, name="pos")
+        yt = keep.tile([P, NJ, HALF], F32, name="yt")
+        ki = keep.tile([P, NJ, HALF], U32, name="ki")
+        kf = keep.tile([P, NJ, HALF], F32, name="kf")
+        ang = keep.tile([P, NJ, 2, HALF], F32, name="ang")
+        sc = keep.tile([P, NJ, 2, HALF], F32, name="sc")
+        ta = keep.tile([P, NJ, 4, HALF], F32, name="ta")
+        tb = keep.tile([P, NJ, 4, HALF], F32, name="tb")
+        gw = keep.tile([P, 2, HS], BF16, name="gw")
+        wsw = keep.tile([P, 2, 2, HALF], BF16, name="wsw")
+        lam = keep.tile([P, 1], BF16, name="lam")
+        cl = keep.tile([P, 1], F32, name="cl")
+        eps_t = keep.tile([P, 1], F32, name="eps_t")
+        junk = keep.tile([P, HS], BF16, name="junk")
+        wz = keep.tile([P, BANK], BF16, name="wz")
+
+        def zero_plane(t):
+            nc.vector.memset(t[:].rearrange("p g n -> p (g n)").bitcast(I32), 0)
+
+        def load_codes(t, src):
+            nc.sync.dma_start(out=t[:].bitcast(I32), in_=src.rearrange("g p n -> p g n").bitcast(I32))
+
+        def load_scales(t, src):
+            for q in range(4):
+                nc.sync.dma_start(
+                    out=t[32 * q : 32 * q + 4, :, :].bitcast(I32),
+                    in_=src[:, 4 * q : 4 * q + 4, :].rearrange("g r n -> r g n").bitcast(I32),
+                )
+
+        def x_cols(b, c, width):
+            return slice(width * (NJ * b + JCH[c][0]), width * (NJ * b + JCH[c][1]))
+
+        def load_x_codes(b, c):
+            load_codes(xc[(b, c)], x_words[:, :, x_cols(b, c, 256)])
+
+        def load_x_scales(b, c):
+            load_scales(xs[(b, c)], x_scales[:, :, x_cols(b, c, P)])
+
+        def load_v1(b, c):
+            nc.sync.dma_start(
+                out=v1c[(b, c)][:],
+                in_=v1f[x_cols(b, c, P), :].rearrange("(n p) d -> p n d", p=P),
+            )
+
+        def w_words(w):
+            if w < 4:
+                return Wq_words[:, :, 2 * BANK * w : 2 * BANK * (w + 1)]
+            return Wkv_words[:, :, 2 * BANK * (w - 4) : 2 * BANK * (w - 3)]
+
+        nc.gpsimd.dma_start(out=gw[:, 0, :], in_=q_scale.partition_broadcast(P))
+        nc.gpsimd.dma_start(out=gw[:, 1, :], in_=k_scale.partition_broadcast(P))
+        nc.gpsimd.dma_start(out=lam[:], in_=value_lambda.partition_broadcast(P))
+        nc.gpsimd.memset(wz[:], 0.0)
+        nc.gpsimd.iota(pos[:], pattern=[[P, NJ]], base=0, channel_multiplier=1, allow_small_or_imprecise_dtypes=True)
+
+        nc.vector.memset(ones[:], 1.0)
+        zero_plane(xs[(0, 0)])
+        zero_plane(ws_a)
+        load_codes(wc[0], w_words(0))
+        load_x_codes(0, 0)
+        load_x_scales(0, 0)
+        load_scales(ws_a, Wq_scales[:, :, 0:BANK])
+
+        nc.scalar.activation(out=junk[:, 0:1], in_=ones[:, 0:1], func=ACT.Sin)
+
+        warm = psum.tile([P, BANK], F32, name="acc", tag="acc")
+        for i in range(N_WARM):
+            nc.tensor.matmul(out=warm[:], lhsT=wz[:, 0:P], rhs=wz[:], start=True, stop=True)
+
+        for m in range(8):
+            nc.vector.tensor_scalar(
+                out=a8[:, m : m + 1], in0=ones[:, m : m + 1],
+                scalar1=THETA ** (-8.0 * m / HALF) / (2.0 * math.pi), scalar2=None, op0=ALU.mult,
+            )
+            nc.scalar.mul(out=b8[:, m : m + 1], in_=ones[:, m : m + 1], mul=THETA ** (-1.0 * m / HALF))
+        zero_plane(ws_b)
+        load_codes(wc[1], w_words(1))
+        load_scales(ws_b, Wq_scales[:, :, BANK : 4 * BANK])
+        load_codes(wc[2], w_words(2))
+        load_codes(wc[3], w_words(3))
+        zero_plane(xs[(1, 0)])
+        load_x_codes(1, 0)
+        load_x_scales(1, 0)
+        zero_plane(ws_kv)
+        load_codes(wc[4], w_words(4))
+        load_scales(ws_kv, Wkv_scales)
+        load_codes(wc[5], w_words(5))
+        load_v1(0, 0)
+        load_v1(1, 0)
+        nc.vector.memset(eps_t[:], EPS)
+        nc.vector.tensor_tensor(
+            out=turn[:].rearrange("p (m n) -> p m n", n=8),
+            in0=a8[:].unsqueeze(2).to_broadcast([P, 8, 8]),
+            in1=b8[:].unsqueeze(1).to_broadcast([P, 8, 8]),
+            op=ALU.mult,
+        )
+
+        def tab_scalar_1(j0, j1):
+            for j in range(j0, j1):
+                nc.scalar.activation(out=yt[:, j, :], in_=turn[:], func=ACT.Copy, scale=pos[:, j : j + 1])
+            nc.scalar.activation(out=ki[:, j0:j1, :], in_=yt[:, j0:j1, :], func=ACT.Copy)
+            nc.scalar.activation(out=kf[:, j0:j1, :], in_=ki[:, j0:j1, :], func=ACT.Copy)
+
+        def tab_vector(j0, j1):
+            y = yt[:, j0:j1, :]
+            e = ang[:, j0:j1, 0, :]
+            nc.vector.tensor_tensor(out=y, in0=y, in1=kf[:, j0:j1, :], op=ALU.subtract)
+            nc.vector.scalar_tensor_tensor(out=e, in0=y, scalar=0.5, in1=y, op0=ALU.is_gt, op1=ALU.subtract)
+            nc.vector.scalar_tensor_tensor(out=kf[:, j0:j1, :], in0=e, scalar=-1.0, in1=e, op0=ALU.mult, op1=ALU.min)
+            nc.vector.tensor_scalar(out=ang[:, j0:j1, 1, :], in0=kf[:, j0:j1, :], scalar1=0.25, scalar2=None, op0=ALU.add)
+
+        def tab_scalar_2(j0, j1):
+            nc.scalar.activation(
+                out=sc[:, j0:j1, :, :].rearrange("p j x i -> p (j x i)"),
+                in_=ang[:, j0:j1, :, :].rearrange("p j x i -> p (j x i)"),
+                func=ACT.Sin, scale=2.0 * math.pi,
+            )
+
+        def tab_products(eng, j0, j1):
+            nj = j1 - j0
+            eng.tensor_tensor(
+                out=ta[:, j0:j1, :, :],
+                in0=sc[:, j0:j1, 1, :].unsqueeze(2).to_broadcast([P, nj, 4, HALF]),
+                in1=gw[:].rearrange("p x (h i) -> p (x h) i", i=HALF).unsqueeze(1).to_broadcast([P, nj, 4, HALF]),
+                op=ALU.mult,
+            )
+            eng.tensor_tensor(
+                out=tb[:, j0:j1, :, :],
+                in0=sc[:, j0:j1, 0, :].unsqueeze(2).to_broadcast([P, nj, 4, HALF]),
+                in1=wsw[:].rearrange("p x h i -> p (x h) i").unsqueeze(1).to_broadcast([P, nj, 4, HALF]),
+                op=ALU.mult,
+            )
+
+        nc.gpsimd.tensor_copy(out=wsw[:, :, 0, :], in_=gw[:, :, HALF:HS])
+        nc.gpsimd.tensor_scalar(out=wsw[:, :, 1, :], in0=gw[:, :, 0:HALF], scalar1=-1.0, scalar2=0.0, op0=ALU.mult, op1=ALU.add)
+
+        tab_scalar_1(*TCH[0])
+        for b in range(NB):
+            zero_plane(xs[(b, 1)])
+            load_x_codes(b, 1)
+            load_x_scales(b, 1)
+            load_v1(b, 1)
+        tab_vector(*TCH[0])
+        tab_scalar_1(*TCH[1])
+        tab_scalar_2(*TCH[0])
+        for b in range(NB):
+            zero_plane(xs[(b, 2)])
+            load_x_codes(b, 2)
+            load_x_scales(b, 2)
+            load_v1(b, 2)
+        tab_products(nc.vector, *TCH[0])
+        nc.vector.tensor_scalar(out=cl[:], in0=lam[:], scalar1=-1.0, scalar2=1.0, op0=ALU.mult, op1=ALU.add)
+        tab_vector(*TCH[1])
+
+        jobs = []
+        for s in range(NB * NJ):
+            for w in range(5):
+                jobs.append((s, w))
+            jobs.append((s, 5))
+        n_jobs = len(jobs)
+
+        def where(s):
+            j, b = s // NB, s % NB
+            c = [i for i in range(len(JCH)) if JCH[i][0] <= j < JCH[i][1]][0]
+            return j, b, c, j - JCH[c][0]
+
+        acc = {}
+        t1 = {}
+        t2 = {}
+        ssq = {}
+        rinv = {}
+        rs_queue = []
+        rs_done = [0]
+
+        def group_of(w):
+            gi = [i for i in range(len(GROUPS)) if w in GROUPS[i]][0]
+            return gi, GROUPS[gi].index(w), len(GROUPS[gi])
+
+        def emit_pe(n):
+            s, w = jobs[n]
+            j, b, c, l = where(s)
+            ps = psum.tile([P, BANK], F32, name="acc", tag="acc")
+            acc[n] = ps
+            for g in range(PASSES):
+                nc.tensor.matmul_mx(
+                    out=ps[:],
+                    lhsT=xc[(b, c)][:, g, 256 * l : 256 * (l + 1)].bitcast(FP4),
+                    lhsT_scale=xs[(b, c)][:, g, P * l : P * (l + 1)],
+                    rhs=wc[w][:, g, :].bitcast(FP4),
+                    rhs_scale=w_plane(w, g),
+                    start=(g == 0),
+                    stop=(g == PASSES - 1),
+                )
+
+        def emit_ss(n):
+            s, w = jobs[n]
+            if w == 5:
+                return
+            gi, bi, nb = group_of(w)
+            if bi == 0:
+                ssq[(s, gi)] = work.tile([P, 4 * nb], F32, name="ss%d" % gi, tag="ss%d" % gi, bufs=4)
+            ps = acc[n]
+            for h in range(4):
+                nc.scalar.activation(
+                    out=junk[:], in_=ps[:, h * HS : (h + 1) * HS], func=ACT.Square,
+                    accum_out=ssq[(s, gi)][:, 4 * bi + h : 4 * bi + h + 1],
+                )
+            if bi == nb - 1:
+                nc.scalar.activation(out=ssq[(s, gi)][:], in_=ssq[(s, gi)][:], func=ACT.Sqrt, scale=1.0 / HS, bias=eps_t[:, 0:1])
+
+        def emit_v(n, step):
+            s, w = jobs[n]
+            j, b, c, l = where(s)
+            tok = P * (NJ * b + j)
+            ps = acc[n]
+            if w == 5:
+                vo = work.tile([P, BANK], F32, name="vo", tag="vo", bufs=4)
+                nc.vector.scalar_tensor_tensor(
+                    out=vo[:], in0=v1c[(b, c)][:, l, :], scalar=cl[:, 0:1], in1=ps[:], op0=ALU.mult, op1=ALU.add
+                )
+                nc.sync.dma_start(out=out2f[tok : tok + P, :], in_=vo[:])
+                return
+            gi, bi, nb = group_of(w)
+            if bi == 0:
+                t1[(s, gi)] = work.tile([P, nb * BANK], F32, name="t1_%d" % gi, tag="t1_%d" % gi, bufs=T1_BUFS)
+                t2[(s, gi)] = work.tile([P, nb * BANK], F32, name="t2_%d" % gi, tag="t2_%d" % gi, bufs=T2_BUFS)
+            x0 = 0 if w < 4 else 2
+            ps3 = ps[:].rearrange("p (h d) -> p h d", h=4)
+            o1 = t1[(s, gi)][:, bi * BANK : (bi + 1) * BANK].rearrange("p (h d) -> p h d", h=4)
+            o2 = t2[(s, gi)][:, bi * BANK : (bi + 1) * BANK].rearrange("p (h d) -> p h d", h=4)
+            nc.vector.tensor_tensor(
+                out=o1, in0=ps3,
+                in1=ta[:, j, x0 : x0 + 2, :].rearrange("p x i -> p (x i)").unsqueeze(1).to_broadcast([P, 4, HS]),
+                op=ALU.mult,
+            )
+            for half in range(2):
+                nc.vector.tensor_tensor(
+                    out=o2[:, :, half * HALF : (half + 1) * HALF],
+                    in0=ps3[:, :, (1 - half) * HALF : (2 - half) * HALF],
+                    in1=tb[:, j, x0 + half, :].unsqueeze(1).to_broadcast([P, 4, HALF]),
+                    op=ALU.mult,
+                )
+            if bi == nb - 1:
+                rinv[(s, gi)] = work.tile([P, 4 * nb], F32, name="ri%d" % gi, tag="ri%d" % gi, bufs=4)
+                nc.vector.reciprocal(out=rinv[(s, gi)][:], in_=ssq[(s, gi)][:])
+                nc.gpsimd.tensor_tensor(out=t1[(s, gi)][:], in0=t1[(s, gi)][:], in1=t2[(s, gi)][:], op=ALU.add)
+                for k in range(nb):
+                    rs_queue.append((step + LAG_RS + k, s, gi, k))
+
+        def emit_rs(s, gi, k):
+            j, b, c, l = where(s)
+            tok = P * (NJ * b + j)
+            nb = len(GROUPS[gi])
+            t = t1[(s, gi)]
+            for h in range(4 * k, 4 * k + 4):
+                nc.scalar.activation(
+                    out=t[:, h * HS : (h + 1) * HS], in_=t[:, h * HS : (h + 1) * HS], func=ACT.Copy,
+                    scale=rinv[(s, gi)][:, h : h + 1],
+                )
+            if k == nb - 1:
+                qb = [w for w in GROUPS[gi] if w < 4]
+                if qb:
+                    nc.sync.dma_start(
+                        out=out0f[tok : tok + P, qb[0] * BANK : (qb[-1] + 1) * BANK], in_=t[:, 0 : len(qb) * BANK]
+                    )
+                if 4 in GROUPS[gi]:
+                    nc.sync.dma_start(out=out1f[tok : tok + P, :], in_=t[:, len(qb) * BANK : (len(qb) + 1) * BANK])
+
+        tab_at = {}
+        for j in range(TCH[1][0], NJ):
+            tab_at[LAG_V + 6 * max(0, NB * (j - 2)) + 5] = tab_at.get(LAG_V + 6 * max(0, NB * (j - 2)) + 5, []) + [j]
+
+        step = 0
+        while step < n_jobs + LAG_V or rs_done[0] < len(rs_queue):
+            if step < n_jobs:
+                emit_pe(step)
+            if 0 <= step - LAG_SS < n_jobs:
+                emit_ss(step - LAG_SS)
+            if step == 2:
+                tab_scalar_2(*TCH[1])
+            while rs_done[0] < len(rs_queue) and rs_queue[rs_done[0]][0] <= step:
+                emit_rs(*rs_queue[rs_done[0]][1:])
+                rs_done[0] += 1
+            if 0 <= step - LAG_V < n_jobs:
+                emit_v(step - LAG_V, step)
+            for j in tab_at.get(step, []):
+                tab_products(nc.gpsimd, j, j + 1)
+            step += 1

@@ -86,7 +86,7 @@ def tile_attention_pa_kernel(
         lam = keep.tile([P, 1], BF16, name="lam")
         cl = keep.tile([P, 1], F32, name="cl")
         eps_t = keep.tile([P, 1], F32, name="eps_t")
-        junk = keep.tile([P, HS], BF16, name="junk")
+        junk = keep.tile([P, 8, HS], BF16, name="junk")
         wz = keep.tile([P, BANK], BF16, name="wz")
 
         def zero_plane(t):
@@ -136,7 +136,7 @@ def tile_attention_pa_kernel(
         load_x_scales(0, 0)
         load_scales(ws_a, Wq_scales[:, :, 0:BANK])
 
-        nc.scalar.activation(out=junk[:, 0:1], in_=ones[:, 0:1], func=ACT.Sin)
+        nc.scalar.activation(out=junk[:, 0, 0:1], in_=ones[:, 0:1], func=ACT.Sin)
 
         warm = psum.tile([P, BANK], F32, name="acc", tag="acc")
         for i in range(N_WARM):
@@ -277,7 +277,7 @@ def tile_attention_pa_kernel(
             ps = acc[n]
             for h in range(4):
                 nc.scalar.activation(
-                    out=junk[:], in_=ps[:, h * HS : (h + 1) * HS], func=ACT.Square,
+                    out=junk[:, 4 * (n % 2) + h, :], in_=ps[:, h * HS : (h + 1) * HS], func=ACT.Square,
                     accum_out=ssq[(s, gi)][:, 4 * bi + h : 4 * bi + h + 1],
                 )
             if bi == nb - 1:
@@ -304,15 +304,16 @@ def tile_attention_pa_kernel(
             o1 = t1[(s, gi)][:, bi * BANK : (bi + 1) * BANK].rearrange("p (h d) -> p h d", h=4)
             o2 = t2[(s, gi)][:, bi * BANK : (bi + 1) * BANK].rearrange("p (h d) -> p h d", h=4)
             nc.vector.tensor_tensor(
-                out=o1, in0=ps3,
-                in1=ta[:, j, x0 : x0 + 2, :].rearrange("p x i -> p (x i)").unsqueeze(1).to_broadcast([P, 4, HS]),
+                out=o1,
+                in0=ta[:, j, x0 : x0 + 2, :].rearrange("p x i -> p (x i)").unsqueeze(1).to_broadcast([P, 4, HS]),
+                in1=ps3,
                 op=ALU.mult,
             )
             for half in range(2):
                 nc.vector.tensor_tensor(
                     out=o2[:, :, half * HALF : (half + 1) * HALF],
-                    in0=ps3[:, :, (1 - half) * HALF : (2 - half) * HALF],
-                    in1=tb[:, j, x0 + half, :].unsqueeze(1).to_broadcast([P, 4, HALF]),
+                    in0=tb[:, j, x0 + half, :].unsqueeze(1).to_broadcast([P, 4, HALF]),
+                    in1=ps3[:, :, (1 - half) * HALF : (2 - half) * HALF],
                     op=ALU.mult,
                 )
             if bi == nb - 1:

@@ -20,18 +20,26 @@ THETA = 10000.0
 P = 128
 PASSES = C // 512
 NJ = T // P
+NT = NB * NJ
 BANK = 512
 FLOPS = 2 * NB * T * C * (NH * HS + 2 * NKV * HS)
 
-JCH = ((0, 2), (2, 6), (6, 12))
-GROUPS = ((0, 1, 2), (3, 4))
-TCH = ((0, 1), (1, 12))
+JCH = ((0, 3), (3, 7), (7, 12))
+TCH = ((0, 6), (6, 12))
+J1 = 3
+W_ORDER1 = (5, 0, 1, 2, 3, 4)
+GSZ = 5
+LAST_SPLIT = (3, 2, 2, 2, 1)
+FUSED = (4,)
+V_TAIL = 5
 LAG_SS = 1
 LAG_V = 2
-LAG_RS = 6
+LAG_RS = {1: 3, 2: 5, 3: 6, 5: 8}
 N_WARM = 10
-T1_BUFS = 4
+T1_BUFS = 5
 T2_BUFS = 3
+TAB_PLAN = (((0, 3), (3, 6)), {14: ((6, 9),), 26: ((9, 12),)})
+LOAD_PLAN = {1: ((3,),), 6: ((4,),), 11: ((5,),), 16: ((0, 1),), 21: ((1, 1),), 50: ((0, 2),), 56: ((1, 2),)}
 
 
 def tile_attention_pa_kernel(
@@ -58,16 +66,7 @@ def tile_attention_pa_kernel(
             xs[(b, c)] = keep.tile([P, PASSES, P * nj], U8, name="xs%d%d" % (b, c), align_bytes=64)
             v1c[(b, c)] = keep.tile([P, nj, BANK], BF16, name="v1c%d%d" % (b, c))
         wc = [keep.tile([P, PASSES, 2 * BANK], U8, name="wc%d" % w, align_bytes=64) for w in range(6)]
-        ws_a = keep.tile([P, PASSES, BANK], U8, name="ws_a", align_bytes=64)
-        ws_b = keep.tile([P, PASSES, 3 * BANK], U8, name="ws_b", align_bytes=64)
-        ws_kv = keep.tile([P, PASSES, 2 * BANK], U8, name="ws_kv", align_bytes=64)
-
-        def w_plane(w, g):
-            if w == 0:
-                return ws_a[:, g, :]
-            if w < 4:
-                return ws_b[:, g, (w - 1) * BANK : w * BANK]
-            return ws_kv[:, g, (w - 4) * BANK : (w - 3) * BANK]
+        ws = [keep.tile([P, PASSES, BANK], U8, name="ws%d" % w, align_bytes=64) for w in range(6)]
 
         ones = keep.tile([P, 8], F32, name="ones")
         a8 = keep.tile([P, 8], F32, name="a8")
@@ -78,7 +77,6 @@ def tile_attention_pa_kernel(
         ki = keep.tile([P, NJ, HALF], U32, name="ki")
         kf = keep.tile([P, NJ, HALF], F32, name="kf")
         ang = keep.tile([P, NJ, 2, HALF], F32, name="ang")
-        sc = keep.tile([P, NJ, 2, HALF], F32, name="sc")
         ta = keep.tile([P, NJ, 4, HALF], F32, name="ta")
         tb = keep.tile([P, NJ, 4, HALF], F32, name="tb")
         gw = keep.tile([P, 2, HS], BF16, name="gw")
@@ -117,11 +115,19 @@ def tile_attention_pa_kernel(
                 in_=v1f[x_cols(b, c, P), :].rearrange("(n p) d -> p n d", p=P),
             )
 
-        def w_words(w):
+        def load_w_codes(w):
             if w < 4:
-                return Wq_words[:, :, 2 * BANK * w : 2 * BANK * (w + 1)]
-            return Wkv_words[:, :, 2 * BANK * (w - 4) : 2 * BANK * (w - 3)]
+                load_codes(wc[w], Wq_words[:, :, 2 * BANK * w : 2 * BANK * (w + 1)])
+            else:
+                load_codes(wc[w], Wkv_words[:, :, 2 * BANK * (w - 4) : 2 * BANK * (w - 3)])
 
+        def load_w_scales(w):
+            if w < 4:
+                load_scales(ws[w], Wq_scales[:, :, BANK * w : BANK * (w + 1)])
+            else:
+                load_scales(ws[w], Wkv_scales[:, :, BANK * (w - 4) : BANK * (w - 3)])
+
+        w_first = W_ORDER1[0]
         nc.gpsimd.dma_start(out=gw[:, 0, :], in_=q_scale.partition_broadcast(P))
         nc.gpsimd.dma_start(out=gw[:, 1, :], in_=k_scale.partition_broadcast(P))
         nc.gpsimd.dma_start(out=lam[:], in_=value_lambda.partition_broadcast(P))
@@ -130,11 +136,11 @@ def tile_attention_pa_kernel(
 
         nc.vector.memset(ones[:], 1.0)
         zero_plane(xs[(0, 0)])
-        zero_plane(ws_a)
-        load_codes(wc[0], w_words(0))
+        zero_plane(ws[w_first])
+        load_w_codes(w_first)
         load_x_codes(0, 0)
         load_x_scales(0, 0)
-        load_scales(ws_a, Wq_scales[:, :, 0:BANK])
+        load_w_scales(w_first)
 
         nc.scalar.activation(out=junk[:, 0, 0:1], in_=ones[:, 0:1], func=ACT.Sin)
 
@@ -148,18 +154,9 @@ def tile_attention_pa_kernel(
                 scalar1=THETA ** (-8.0 * m / HALF) / (2.0 * math.pi), scalar2=None, op0=ALU.mult,
             )
             nc.scalar.mul(out=b8[:, m : m + 1], in_=ones[:, m : m + 1], mul=THETA ** (-1.0 * m / HALF))
-        zero_plane(ws_b)
-        load_codes(wc[1], w_words(1))
-        load_scales(ws_b, Wq_scales[:, :, BANK : 4 * BANK])
-        load_codes(wc[2], w_words(2))
-        load_codes(wc[3], w_words(3))
         zero_plane(xs[(1, 0)])
         load_x_codes(1, 0)
         load_x_scales(1, 0)
-        zero_plane(ws_kv)
-        load_codes(wc[4], w_words(4))
-        load_scales(ws_kv, Wkv_scales)
-        load_codes(wc[5], w_words(5))
         load_v1(0, 0)
         load_v1(1, 0)
         nc.vector.memset(eps_t[:], EPS)
@@ -185,23 +182,20 @@ def tile_attention_pa_kernel(
             nc.vector.tensor_scalar(out=ang[:, j0:j1, 1, :], in0=kf[:, j0:j1, :], scalar1=0.25, scalar2=None, op0=ALU.add)
 
         def tab_scalar_2(j0, j1):
-            nc.scalar.activation(
-                out=sc[:, j0:j1, :, :].rearrange("p j x i -> p (j x i)"),
-                in_=ang[:, j0:j1, :, :].rearrange("p j x i -> p (j x i)"),
-                func=ACT.Sin, scale=2.0 * math.pi,
-            )
+            a = ang[:, j0:j1, :, :].rearrange("p j x i -> p (j x i)")
+            nc.scalar.activation(out=a, in_=a, func=ACT.Sin, scale=2.0 * math.pi)
 
-        def tab_products(eng, j0, j1):
+        def tab_products(j0, j1):
             nj = j1 - j0
-            eng.tensor_tensor(
+            nc.gpsimd.tensor_tensor(
                 out=ta[:, j0:j1, :, :],
-                in0=sc[:, j0:j1, 1, :].unsqueeze(2).to_broadcast([P, nj, 4, HALF]),
+                in0=ang[:, j0:j1, 1, :].unsqueeze(2).to_broadcast([P, nj, 4, HALF]),
                 in1=gw[:].rearrange("p x (h i) -> p (x h) i", i=HALF).unsqueeze(1).to_broadcast([P, nj, 4, HALF]),
                 op=ALU.mult,
             )
-            eng.tensor_tensor(
+            nc.gpsimd.tensor_tensor(
                 out=tb[:, j0:j1, :, :],
-                in0=sc[:, j0:j1, 0, :].unsqueeze(2).to_broadcast([P, nj, 4, HALF]),
+                in0=ang[:, j0:j1, 0, :].unsqueeze(2).to_broadcast([P, nj, 4, HALF]),
                 in1=wsw[:].rearrange("p x h i -> p (x h) i").unsqueeze(1).to_broadcast([P, nj, 4, HALF]),
                 op=ALU.mult,
             )
@@ -209,35 +203,64 @@ def tile_attention_pa_kernel(
         nc.gpsimd.tensor_copy(out=wsw[:, :, 0, :], in_=gw[:, :, HALF:HS])
         nc.gpsimd.tensor_scalar(out=wsw[:, :, 1, :], in0=gw[:, :, 0:HALF], scalar1=-1.0, scalar2=0.0, op0=ALU.mult, op1=ALU.add)
 
+        def load_w(w):
+            load_w_codes(w)
+            load_w_scales(w)
+
+        def load_x(b, c):
+            load_x_codes(b, c)
+            load_x_scales(b, c)
+            load_v1(b, c)
+
         tab_scalar_1(*TCH[0])
-        for b in range(NB):
-            zero_plane(xs[(b, 1)])
-            load_x_codes(b, 1)
-            load_x_scales(b, 1)
-            load_v1(b, 1)
+        for w in W_ORDER1[1:4]:
+            zero_plane(ws[w])
+        load_w(W_ORDER1[1])
         tab_vector(*TCH[0])
         tab_scalar_1(*TCH[1])
         tab_scalar_2(*TCH[0])
-        for b in range(NB):
-            zero_plane(xs[(b, 2)])
-            load_x_codes(b, 2)
-            load_x_scales(b, 2)
-            load_v1(b, 2)
-        tab_products(nc.vector, *TCH[0])
-        nc.vector.tensor_scalar(out=cl[:], in0=lam[:], scalar1=-1.0, scalar2=1.0, op0=ALU.mult, op1=ALU.add)
+        for w in W_ORDER1[4:]:
+            zero_plane(ws[w])
+        for c in range(1, len(JCH)):
+            for b in range(NB):
+                zero_plane(xs[(b, c)])
+        load_w(W_ORDER1[2])
         tab_vector(*TCH[1])
+        tab_scalar_2(*TCH[1])
+        nc.scalar.activation(out=junk[:, 0, 0:1], in_=ones[:, 0:1], func=ACT.Abs_reciprocal_sqrt)
+        nc.vector.tensor_scalar(out=cl[:], in0=lam[:], scalar1=-1.0, scalar2=1.0, op0=ALU.mult, op1=ALU.add)
+        for j0, j1 in TAB_PLAN[0]:
+            tab_products(j0, j1)
 
         jobs = []
-        for s in range(NB * NJ):
+        for w in W_ORDER1:
+            for b in range(NB):
+                for j in range(J1):
+                    jobs.append((j, b, w))
+        rest = [(j, b) for j in range(J1, NJ) for b in range(NB)]
+        for i in range(len(rest)):
             for w in range(5):
-                jobs.append((s, w))
-            jobs.append((s, 5))
+                jobs.append(rest[i] + (w,))
+            if i < len(rest) - V_TAIL:
+                jobs.append(rest[i] + (5,))
+        for i in range(len(rest) - V_TAIL, len(rest)):
+            jobs.append(rest[i] + (5,))
         n_jobs = len(jobs)
 
-        def where(s):
-            j, b = s // NB, s % NB
+        qk = [n for n in range(n_jobs) if jobs[n][2] != 5]
+        sizes = [GSZ] * ((len(qk) - sum(LAST_SPLIT)) // GSZ) + list(LAST_SPLIT)
+        assert sum(sizes) == len(qk)
+        groups = []
+        place = {}
+        for size in sizes:
+            first = sum(len(g) for g in groups)
+            groups.append(qk[first : first + size])
+            for i in range(size):
+                place[qk[first + i]] = (len(groups) - 1, i)
+
+        def chunk_of(j):
             c = [i for i in range(len(JCH)) if JCH[i][0] <= j < JCH[i][1]][0]
-            return j, b, c, j - JCH[c][0]
+            return c, j - JCH[c][0]
 
         acc = {}
         t1 = {}
@@ -247,13 +270,9 @@ def tile_attention_pa_kernel(
         rs_queue = []
         rs_done = [0]
 
-        def group_of(w):
-            gi = [i for i in range(len(GROUPS)) if w in GROUPS[i]][0]
-            return gi, GROUPS[gi].index(w), len(GROUPS[gi])
-
         def emit_pe(n):
-            s, w = jobs[n]
-            j, b, c, l = where(s)
+            j, b, w = jobs[n]
+            c, l = chunk_of(j)
             ps = psum.tile([P, BANK], F32, name="acc", tag="acc")
             acc[n] = ps
             for g in range(PASSES):
@@ -262,103 +281,145 @@ def tile_attention_pa_kernel(
                     lhsT=xc[(b, c)][:, g, 256 * l : 256 * (l + 1)].bitcast(FP4),
                     lhsT_scale=xs[(b, c)][:, g, P * l : P * (l + 1)],
                     rhs=wc[w][:, g, :].bitcast(FP4),
-                    rhs_scale=w_plane(w, g),
+                    rhs_scale=ws[w][:, g, :],
                     start=(g == 0),
                     stop=(g == PASSES - 1),
                 )
 
         def emit_ss(n):
-            s, w = jobs[n]
+            j, b, w = jobs[n]
             if w == 5:
                 return
-            gi, bi, nb = group_of(w)
+            gi, bi = place[n]
+            grp = groups[gi]
             if bi == 0:
-                ssq[(s, gi)] = work.tile([P, 4 * nb], F32, name="ss%d" % gi, tag="ss%d" % gi, bufs=4)
+                ssq[gi] = work.tile([P, 4 * GSZ], F32, name="ss", tag="ss", bufs=6)
+                rinv[gi] = work.tile([P, 4 * GSZ], F32, name="ri", tag="ri", bufs=10)
             ps = acc[n]
             for h in range(4):
                 nc.scalar.activation(
                     out=junk[:, 4 * (n % 2) + h, :], in_=ps[:, h * HS : (h + 1) * HS], func=ACT.Square,
-                    accum_out=ssq[(s, gi)][:, 4 * bi + h : 4 * bi + h + 1],
+                    accum_out=ssq[gi][:, 4 * bi + h : 4 * bi + h + 1],
                 )
-            if bi == nb - 1:
-                nc.scalar.activation(out=ssq[(s, gi)][:], in_=ssq[(s, gi)][:], func=ACT.Sqrt, scale=1.0 / HS, bias=eps_t[:, 0:1])
+            b0 = bi
+            if w not in FUSED:
+                if bi + 1 < len(grp) and jobs[grp[bi + 1]][2] not in FUSED:
+                    return
+                while b0 > 0 and jobs[grp[b0 - 1]][2] not in FUSED:
+                    b0 -= 1
+            nc.scalar.activation(
+                out=rinv[gi][:, 4 * b0 : 4 * bi + 4], in_=ssq[gi][:, 4 * b0 : 4 * bi + 4], func=ACT.Abs_reciprocal_sqrt,
+                scale=1.0 / HS, bias=eps_t[:, 0:1],
+            )
+
+        def store_banks(gi, banks):
+            t = t1[gi]
+            i = 0
+            while i < len(banks):
+                j, b, w = jobs[groups[gi][banks[i]]]
+                k = i
+                while (
+                    k + 1 < len(banks) and banks[k + 1] == banks[k] + 1 and w + k + 1 - i < 4
+                    and jobs[groups[gi][banks[k + 1]]] == (j, b, w + k + 1 - i)
+                ):
+                    k += 1
+                tok = P * (NJ * b + j)
+                src = t[:, banks[i] * BANK : (banks[k] + 1) * BANK]
+                if w < 4:
+                    nc.sync.dma_start(out=out0f[tok : tok + P, w * BANK : (w + k + 1 - i) * BANK], in_=src)
+                else:
+                    nc.sync.dma_start(out=out1f[tok : tok + P, :], in_=src)
+                i = k + 1
 
         def emit_v(n, step):
-            s, w = jobs[n]
-            j, b, c, l = where(s)
+            j, b, w = jobs[n]
+            c, l = chunk_of(j)
             tok = P * (NJ * b + j)
             ps = acc[n]
             if w == 5:
-                vo = work.tile([P, BANK], F32, name="vo", tag="vo", bufs=4)
+                vo = work.tile([P, BANK], F32, name="vo", tag="vo", bufs=6)
                 nc.vector.scalar_tensor_tensor(
                     out=vo[:], in0=v1c[(b, c)][:, l, :], scalar=cl[:, 0:1], in1=ps[:], op0=ALU.mult, op1=ALU.add
                 )
                 nc.sync.dma_start(out=out2f[tok : tok + P, :], in_=vo[:])
                 return
-            gi, bi, nb = group_of(w)
+            gi, bi = place[n]
+            grp = groups[gi]
+            nb = len(grp)
             if bi == 0:
-                t1[(s, gi)] = work.tile([P, nb * BANK], F32, name="t1_%d" % gi, tag="t1_%d" % gi, bufs=T1_BUFS)
-                t2[(s, gi)] = work.tile([P, nb * BANK], F32, name="t2_%d" % gi, tag="t2_%d" % gi, bufs=T2_BUFS)
+                t1[gi] = work.tile([P, nb * BANK], F32, name="t1", tag="t1", bufs=T1_BUFS)
+                t2[gi] = work.tile([P, nb * BANK], F32, name="t2", tag="t2", bufs=T2_BUFS)
             x0 = 0 if w < 4 else 2
             ps3 = ps[:].rearrange("p (h d) -> p h d", h=4)
-            o1 = t1[(s, gi)][:, bi * BANK : (bi + 1) * BANK].rearrange("p (h d) -> p h d", h=4)
-            o2 = t2[(s, gi)][:, bi * BANK : (bi + 1) * BANK].rearrange("p (h d) -> p h d", h=4)
-            nc.vector.tensor_tensor(
-                out=o1,
-                in0=ta[:, j, x0 : x0 + 2, :].rearrange("p x i -> p (x i)").unsqueeze(1).to_broadcast([P, 4, HS]),
-                in1=ps3,
-                op=ALU.mult,
-            )
-            for half in range(2):
+            o1 = t1[gi][:, bi * BANK : (bi + 1) * BANK].rearrange("p (h d) -> p h d", h=4)
+            o2 = t2[gi][:, bi * BANK : (bi + 1) * BANK].rearrange("p (h d) -> p h d", h=4)
+            if w in FUSED:
+                for h in range(4):
+                    r = rinv[gi][:, 4 * bi + h : 4 * bi + h + 1]
+                    nc.vector.scalar_tensor_tensor(
+                        out=o1[:, h, :], in0=ta[:, j, x0 : x0 + 2, :].rearrange("p x i -> p (x i)"), scalar=r,
+                        in1=ps3[:, h, :], op0=ALU.mult, op1=ALU.mult,
+                    )
+                    for half in range(2):
+                        nc.vector.scalar_tensor_tensor(
+                            out=o2[:, h, half * HALF : (half + 1) * HALF], in0=tb[:, j, x0 + half, :], scalar=r,
+                            in1=ps3[:, h, (1 - half) * HALF : (2 - half) * HALF], op0=ALU.mult, op1=ALU.mult,
+                        )
+            else:
                 nc.vector.tensor_tensor(
-                    out=o2[:, :, half * HALF : (half + 1) * HALF],
-                    in0=tb[:, j, x0 + half, :].unsqueeze(1).to_broadcast([P, 4, HALF]),
-                    in1=ps3[:, :, (1 - half) * HALF : (2 - half) * HALF],
+                    out=o1,
+                    in0=ta[:, j, x0 : x0 + 2, :].rearrange("p x i -> p (x i)").unsqueeze(1).to_broadcast([P, 4, HS]),
+                    in1=ps3,
                     op=ALU.mult,
                 )
-            if bi == nb - 1:
-                rinv[(s, gi)] = work.tile([P, 4 * nb], F32, name="ri%d" % gi, tag="ri%d" % gi, bufs=4)
-                nc.vector.reciprocal(out=rinv[(s, gi)][:], in_=ssq[(s, gi)][:])
-                nc.gpsimd.tensor_tensor(out=t1[(s, gi)][:], in0=t1[(s, gi)][:], in1=t2[(s, gi)][:], op=ALU.add)
-                for k in range(nb):
-                    rs_queue.append((step + LAG_RS + k, s, gi, k))
-
-        def emit_rs(s, gi, k):
-            j, b, c, l = where(s)
-            tok = P * (NJ * b + j)
-            nb = len(GROUPS[gi])
-            t = t1[(s, gi)]
-            for h in range(4 * k, 4 * k + 4):
-                nc.scalar.activation(
-                    out=t[:, h * HS : (h + 1) * HS], in_=t[:, h * HS : (h + 1) * HS], func=ACT.Copy,
-                    scale=rinv[(s, gi)][:, h : h + 1],
-                )
-            if k == nb - 1:
-                qb = [w for w in GROUPS[gi] if w < 4]
-                if qb:
-                    nc.sync.dma_start(
-                        out=out0f[tok : tok + P, qb[0] * BANK : (qb[-1] + 1) * BANK], in_=t[:, 0 : len(qb) * BANK]
+                for half in range(2):
+                    nc.vector.tensor_tensor(
+                        out=o2[:, :, half * HALF : (half + 1) * HALF],
+                        in0=tb[:, j, x0 + half, :].unsqueeze(1).to_broadcast([P, 4, HALF]),
+                        in1=ps3[:, :, (1 - half) * HALF : (2 - half) * HALF],
+                        op=ALU.mult,
                     )
-                if 4 in GROUPS[gi]:
-                    nc.sync.dma_start(out=out1f[tok : tok + P, :], in_=t[:, len(qb) * BANK : (len(qb) + 1) * BANK])
+            if bi == nb - 1:
+                nc.gpsimd.tensor_tensor(out=t1[gi][:], in0=t1[gi][:], in1=t2[gi][:], op=ALU.add)
+                lag = LAG_RS[nb]
+                rs_queue.append((step + lag, gi, -1))
+                k = 0
+                for i in range(nb):
+                    if jobs[grp[i]][2] not in FUSED:
+                        rs_queue.append((step + lag + k, gi, i))
+                        k += 1
+                rs_queue.append((step + lag + max(0, k - 1), gi, -2))
 
-        tab_at = {}
-        for j in range(TCH[1][0], NJ):
-            tab_at[LAG_V + 6 * max(0, NB * (j - 2)) + 5] = tab_at.get(LAG_V + 6 * max(0, NB * (j - 2)) + 5, []) + [j]
+        def emit_rs(gi, i):
+            grp = groups[gi]
+            t = t1[gi]
+            if i == -1:
+                store_banks(gi, [k for k in range(len(grp)) if jobs[grp[k]][2] in FUSED])
+            elif i == -2:
+                store_banks(gi, [k for k in range(len(grp)) if jobs[grp[k]][2] not in FUSED])
+            else:
+                for h in range(4 * i, 4 * i + 4):
+                    nc.scalar.activation(
+                        out=t[:, h * HS : (h + 1) * HS], in_=t[:, h * HS : (h + 1) * HS], func=ACT.Copy,
+                        scale=rinv[gi][:, h : h + 1],
+                    )
 
         step = 0
         while step < n_jobs + LAG_V or rs_done[0] < len(rs_queue):
+            for what in LOAD_PLAN.get(step, ()):
+                if len(what) == 1:
+                    load_w(W_ORDER1[what[0]])
+                else:
+                    load_x(*what)
             if step < n_jobs:
                 emit_pe(step)
             if 0 <= step - LAG_SS < n_jobs:
                 emit_ss(step - LAG_SS)
-            if step == 2:
-                tab_scalar_2(*TCH[1])
             while rs_done[0] < len(rs_queue) and rs_queue[rs_done[0]][0] <= step:
                 emit_rs(*rs_queue[rs_done[0]][1:])
                 rs_done[0] += 1
             if 0 <= step - LAG_V < n_jobs:
                 emit_v(step - LAG_V, step)
-            for j in tab_at.get(step, []):
-                tab_products(nc.gpsimd, j, j + 1)
+            for j0, j1 in TAB_PLAN[1].get(step, ()):
+                tab_products(j0, j1)
             step += 1

@@ -28,17 +28,18 @@ JCH = ((0, 3), (3, 7), (7, 12))
 TCH = ((0, 6), (6, 12))
 J1 = 3
 W_ORDER1 = (5, 0, 1, 2, 3, 4)
-GSZ = 5
-LAST_SPLIT = (3, 2, 2, 2, 1)
-FUSED = (4,)
+GSZ = 3
+LAST_SPLIT = (2, 1)
+FUSED = (3, 4)
 V_TAIL = 5
+N_LATE = 0
 LAG_SS = 1
 LAG_V = 2
-LAG_RS = {1: 3, 2: 5, 3: 6, 5: 8}
+LAG_RS = {1: 4, 2: 6, 3: 8, 4: 9, 5: 11}
 N_WARM = 10
-T1_BUFS = 5
-T2_BUFS = 3
-TAB_PLAN = (((0, 3), (3, 6)), {14: ((6, 9),), 26: ((9, 12),)})
+T1_BUFS = 8
+T2_BUFS = 5
+TAB_PLAN = (((6, 12),), {}, ((0, 6),))
 LOAD_PLAN = {1: ((3,),), 6: ((4,),), 11: ((5,),), 16: ((0, 1),), 21: ((1, 1),), 50: ((0, 2),), 56: ((1, 2),)}
 
 
@@ -185,15 +186,15 @@ def tile_attention_pa_kernel(
             a = ang[:, j0:j1, :, :].rearrange("p j x i -> p (j x i)")
             nc.scalar.activation(out=a, in_=a, func=ACT.Sin, scale=2.0 * math.pi)
 
-        def tab_products(j0, j1):
+        def tab_products(j0, j1, eng=nc.gpsimd):
             nj = j1 - j0
-            nc.gpsimd.tensor_tensor(
+            eng.tensor_tensor(
                 out=ta[:, j0:j1, :, :],
                 in0=ang[:, j0:j1, 1, :].unsqueeze(2).to_broadcast([P, nj, 4, HALF]),
                 in1=gw[:].rearrange("p x (h i) -> p (x h) i", i=HALF).unsqueeze(1).to_broadcast([P, nj, 4, HALF]),
                 op=ALU.mult,
             )
-            nc.gpsimd.tensor_tensor(
+            eng.tensor_tensor(
                 out=tb[:, j0:j1, :, :],
                 in0=ang[:, j0:j1, 0, :].unsqueeze(2).to_broadcast([P, nj, 4, HALF]),
                 in1=wsw[:].rearrange("p x h i -> p (x h) i").unsqueeze(1).to_broadcast([P, nj, 4, HALF]),
@@ -229,6 +230,8 @@ def tile_attention_pa_kernel(
         tab_scalar_2(*TCH[1])
         nc.scalar.activation(out=junk[:, 0, 0:1], in_=ones[:, 0:1], func=ACT.Abs_reciprocal_sqrt)
         nc.vector.tensor_scalar(out=cl[:], in0=lam[:], scalar1=-1.0, scalar2=1.0, op0=ALU.mult, op1=ALU.add)
+        for j0, j1 in TAB_PLAN[2]:
+            tab_products(j0, j1, nc.vector)
         for j0, j1 in TAB_PLAN[0]:
             tab_products(j0, j1)
 
@@ -246,6 +249,8 @@ def tile_attention_pa_kernel(
         for i in range(len(rest) - V_TAIL, len(rest)):
             jobs.append(rest[i] + (5,))
         n_jobs = len(jobs)
+        late = rest[len(rest) - N_LATE :] if N_LATE else []
+        fused_job = [(w in FUSED or (j, b) in late) and w != 5 for j, b, w in jobs]
 
         qk = [n for n in range(n_jobs) if jobs[n][2] != 5]
         sizes = [GSZ] * ((len(qk) - sum(LAST_SPLIT)) // GSZ) + list(LAST_SPLIT)
@@ -302,10 +307,10 @@ def tile_attention_pa_kernel(
                     accum_out=ssq[gi][:, 4 * bi + h : 4 * bi + h + 1],
                 )
             b0 = bi
-            if w not in FUSED:
-                if bi + 1 < len(grp) and jobs[grp[bi + 1]][2] not in FUSED:
+            if not fused_job[n]:
+                if bi + 1 < len(grp) and not fused_job[grp[bi + 1]]:
                     return
-                while b0 > 0 and jobs[grp[b0 - 1]][2] not in FUSED:
+                while b0 > 0 and not fused_job[grp[b0 - 1]]:
                     b0 -= 1
             nc.scalar.activation(
                 out=rinv[gi][:, 4 * b0 : 4 * bi + 4], in_=ssq[gi][:, 4 * b0 : 4 * bi + 4], func=ACT.Abs_reciprocal_sqrt,
@@ -353,7 +358,7 @@ def tile_attention_pa_kernel(
             ps3 = ps[:].rearrange("p (h d) -> p h d", h=4)
             o1 = t1[gi][:, bi * BANK : (bi + 1) * BANK].rearrange("p (h d) -> p h d", h=4)
             o2 = t2[gi][:, bi * BANK : (bi + 1) * BANK].rearrange("p (h d) -> p h d", h=4)
-            if w in FUSED:
+            if fused_job[n]:
                 for h in range(4):
                     r = rinv[gi][:, 4 * bi + h : 4 * bi + h + 1]
                     nc.vector.scalar_tensor_tensor(
@@ -385,7 +390,7 @@ def tile_attention_pa_kernel(
                 rs_queue.append((step + lag, gi, -1))
                 k = 0
                 for i in range(nb):
-                    if jobs[grp[i]][2] not in FUSED:
+                    if not fused_job[grp[i]]:
                         rs_queue.append((step + lag + k, gi, i))
                         k += 1
                 rs_queue.append((step + lag + max(0, k - 1), gi, -2))
@@ -394,9 +399,9 @@ def tile_attention_pa_kernel(
             grp = groups[gi]
             t = t1[gi]
             if i == -1:
-                store_banks(gi, [k for k in range(len(grp)) if jobs[grp[k]][2] in FUSED])
+                store_banks(gi, [k for k in range(len(grp)) if fused_job[grp[k]]])
             elif i == -2:
-                store_banks(gi, [k for k in range(len(grp)) if jobs[grp[k]][2] not in FUSED])
+                store_banks(gi, [k for k in range(len(grp)) if not fused_job[grp[k]]])
             else:
                 for h in range(4 * i, 4 * i + 4):
                     nc.scalar.activation(

@@ -30,13 +30,13 @@ J1 = 3
 W_ORDER1 = (5, 0, 1, 2, 3, 4)
 GSZ = 3
 LAST_SPLIT = (2, 1)
-FUSED = (3, 4)
-V_TAIL = 5
+FUSED = (2, 3, 4)
+V_TAIL = 7
 N_LATE = 0
 LAG_SS = 1
 LAG_V = 2
-LAG_RS = {1: 4, 2: 6, 3: 8, 4: 9, 5: 11}
-N_WARM = 10
+LAG_RS = {1: 3, 2: 5, 3: 7}
+N_WARM = 15
 T1_BUFS = 8
 T2_BUFS = 5
 TAB_PLAN = (((6, 12),), {}, ((0, 6),))
@@ -77,11 +77,12 @@ def tile_attention_pa_kernel(
         yt = keep.tile([P, NJ, HALF], F32, name="yt")
         ki = keep.tile([P, NJ, HALF], U32, name="ki")
         kf = keep.tile([P, NJ, HALF], F32, name="kf")
-        ang = keep.tile([P, NJ, 2, HALF], F32, name="ang")
-        ta = keep.tile([P, NJ, 4, HALF], F32, name="ta")
-        tb = keep.tile([P, NJ, 4, HALF], F32, name="tb")
+        ang = keep.tile([P, NJ, 3, HALF], F32, name="ang")
+        t_lo = keep.tile([P, NJ, 2, HS], F32, name="t_lo")
+        t_hi = keep.tile([P, NJ, 2, HS], F32, name="t_hi")
         gw = keep.tile([P, 2, HS], BF16, name="gw")
-        wsw = keep.tile([P, 2, 2, HALF], BF16, name="wsw")
+        w_lo = keep.tile([P, 2, 2, HALF], BF16, name="w_lo")
+        w_hi = keep.tile([P, 2, 2, HALF], BF16, name="w_hi")
         lam = keep.tile([P, 1], BF16, name="lam")
         cl = keep.tile([P, 1], F32, name="cl")
         eps_t = keep.tile([P, 1], F32, name="eps_t")
@@ -129,11 +130,11 @@ def tile_attention_pa_kernel(
                 load_scales(ws[w], Wkv_scales[:, :, BANK * (w - 4) : BANK * (w - 3)])
 
         w_first = W_ORDER1[0]
+        nc.gpsimd.memset(wz[:], 0.0)
+        nc.gpsimd.iota(pos[:], pattern=[[P, NJ]], base=0, channel_multiplier=1, allow_small_or_imprecise_dtypes=True)
         nc.gpsimd.dma_start(out=gw[:, 0, :], in_=q_scale.partition_broadcast(P))
         nc.gpsimd.dma_start(out=gw[:, 1, :], in_=k_scale.partition_broadcast(P))
         nc.gpsimd.dma_start(out=lam[:], in_=value_lambda.partition_broadcast(P))
-        nc.gpsimd.memset(wz[:], 0.0)
-        nc.gpsimd.iota(pos[:], pattern=[[P, NJ]], base=0, channel_multiplier=1, allow_small_or_imprecise_dtypes=True)
 
         nc.vector.memset(ones[:], 1.0)
         zero_plane(xs[(0, 0)])
@@ -150,10 +151,7 @@ def tile_attention_pa_kernel(
             nc.tensor.matmul(out=warm[:], lhsT=wz[:, 0:P], rhs=wz[:], start=True, stop=True)
 
         for m in range(8):
-            nc.vector.tensor_scalar(
-                out=a8[:, m : m + 1], in0=ones[:, m : m + 1],
-                scalar1=THETA ** (-8.0 * m / HALF) / (2.0 * math.pi), scalar2=None, op0=ALU.mult,
-            )
+            nc.scalar.mul(out=a8[:, m : m + 1], in_=ones[:, m : m + 1], mul=THETA ** (-8.0 * m / HALF) / (2.0 * math.pi))
             nc.scalar.mul(out=b8[:, m : m + 1], in_=ones[:, m : m + 1], mul=THETA ** (-1.0 * m / HALF))
         zero_plane(xs[(1, 0)])
         load_x_codes(1, 0)
@@ -179,30 +177,28 @@ def tile_attention_pa_kernel(
             e = ang[:, j0:j1, 0, :]
             nc.vector.tensor_tensor(out=y, in0=y, in1=kf[:, j0:j1, :], op=ALU.subtract)
             nc.vector.scalar_tensor_tensor(out=e, in0=y, scalar=0.5, in1=y, op0=ALU.is_gt, op1=ALU.subtract)
-            nc.vector.scalar_tensor_tensor(out=kf[:, j0:j1, :], in0=e, scalar=-1.0, in1=e, op0=ALU.mult, op1=ALU.min)
-            nc.vector.tensor_scalar(out=ang[:, j0:j1, 1, :], in0=kf[:, j0:j1, :], scalar1=0.25, scalar2=None, op0=ALU.add)
+
 
         def tab_scalar_2(j0, j1):
+            e = ang[:, j0:j1, 0, :]
+            nc.scalar.activation(out=kf[:, j0:j1, :], in_=e, func=ACT.Abs)
+            nc.scalar.activation(out=ang[:, j0:j1, 1, :], in_=kf[:, j0:j1, :], func=ACT.Copy, scale=-1.0, bias=0.25)
+            nc.scalar.mul(out=ang[:, j0:j1, 2, :], in_=e, mul=-1.0)
             a = ang[:, j0:j1, :, :].rearrange("p j x i -> p (j x i)")
             nc.scalar.activation(out=a, in_=a, func=ACT.Sin, scale=2.0 * math.pi)
 
         def tab_products(j0, j1, eng=nc.gpsimd):
             nj = j1 - j0
-            eng.tensor_tensor(
-                out=ta[:, j0:j1, :, :],
-                in0=ang[:, j0:j1, 1, :].unsqueeze(2).to_broadcast([P, nj, 4, HALF]),
-                in1=gw[:].rearrange("p x (h i) -> p (x h) i", i=HALF).unsqueeze(1).to_broadcast([P, nj, 4, HALF]),
-                op=ALU.mult,
-            )
-            eng.tensor_tensor(
-                out=tb[:, j0:j1, :, :],
-                in0=ang[:, j0:j1, 0, :].unsqueeze(2).to_broadcast([P, nj, 4, HALF]),
-                in1=wsw[:].rearrange("p x h i -> p (x h) i").unsqueeze(1).to_broadcast([P, nj, 4, HALF]),
-                op=ALU.mult,
-            )
+            for tab, first, gain in ((t_lo, 1, w_lo), (t_hi, 0, w_hi)):
+                eng.tensor_tensor(
+                    out=tab[:, j0:j1, :, :],
+                    in0=ang[:, j0:j1, first : first + 2, :].rearrange("p j x i -> p j (x i)").unsqueeze(2).to_broadcast([P, nj, 2, HS]),
+                    in1=gain[:].rearrange("p k x i -> p k (x i)").unsqueeze(1).to_broadcast([P, nj, 2, HS]),
+                    op=ALU.mult,
+                )
 
-        nc.gpsimd.tensor_copy(out=wsw[:, :, 0, :], in_=gw[:, :, HALF:HS])
-        nc.gpsimd.tensor_scalar(out=wsw[:, :, 1, :], in0=gw[:, :, 0:HALF], scalar1=-1.0, scalar2=0.0, op0=ALU.mult, op1=ALU.add)
+        nc.gpsimd.tensor_copy(out=w_lo[:], in_=gw[:, :, 0:HALF].unsqueeze(2).to_broadcast([P, 2, 2, HALF]))
+        nc.gpsimd.tensor_copy(out=w_hi[:], in_=gw[:, :, HALF:HS].unsqueeze(2).to_broadcast([P, 2, 2, HALF]))
 
         def load_w(w):
             load_w_codes(w)
@@ -354,34 +350,25 @@ def tile_attention_pa_kernel(
             if bi == 0:
                 t1[gi] = work.tile([P, nb * BANK], F32, name="t1", tag="t1", bufs=T1_BUFS)
                 t2[gi] = work.tile([P, nb * BANK], F32, name="t2", tag="t2", bufs=T2_BUFS)
-            x0 = 0 if w < 4 else 2
+            kind = 0 if w < 4 else 1
             ps3 = ps[:].rearrange("p (h d) -> p h d", h=4)
-            o1 = t1[gi][:, bi * BANK : (bi + 1) * BANK].rearrange("p (h d) -> p h d", h=4)
-            o2 = t2[gi][:, bi * BANK : (bi + 1) * BANK].rearrange("p (h d) -> p h d", h=4)
-            if fused_job[n]:
-                for h in range(4):
-                    r = rinv[gi][:, 4 * bi + h : 4 * bi + h + 1]
-                    nc.vector.scalar_tensor_tensor(
-                        out=o1[:, h, :], in0=ta[:, j, x0 : x0 + 2, :].rearrange("p x i -> p (x i)"), scalar=r,
-                        in1=ps3[:, h, :], op0=ALU.mult, op1=ALU.mult,
-                    )
-                    for half in range(2):
+            parts = (
+                (t1[gi], t_lo[:, j, kind, :].rearrange("p (x i) -> p x i", x=2), 0),
+                (t2[gi], t_hi[:, j, kind, :].rearrange("p (x i) -> p x i", x=2), HALF),
+            )
+            for dst, tab, d0 in parts:
+                o = dst[:, bi * BANK : (bi + 1) * BANK].rearrange("p (h x i) -> p h x i", h=4, x=2)
+                if fused_job[n]:
+                    for h in range(4):
                         nc.vector.scalar_tensor_tensor(
-                            out=o2[:, h, half * HALF : (half + 1) * HALF], in0=tb[:, j, x0 + half, :], scalar=r,
-                            in1=ps3[:, h, (1 - half) * HALF : (2 - half) * HALF], op0=ALU.mult, op1=ALU.mult,
+                            out=o[:, h, :, :], in0=tab, scalar=rinv[gi][:, 4 * bi + h : 4 * bi + h + 1],
+                            in1=ps3[:, h, d0 : d0 + HALF].unsqueeze(1).to_broadcast([P, 2, HALF]),
+                            op0=ALU.mult, op1=ALU.mult,
                         )
-            else:
-                nc.vector.tensor_tensor(
-                    out=o1,
-                    in0=ta[:, j, x0 : x0 + 2, :].rearrange("p x i -> p (x i)").unsqueeze(1).to_broadcast([P, 4, HS]),
-                    in1=ps3,
-                    op=ALU.mult,
-                )
-                for half in range(2):
+                else:
                     nc.vector.tensor_tensor(
-                        out=o2[:, :, half * HALF : (half + 1) * HALF],
-                        in0=tb[:, j, x0 + half, :].unsqueeze(1).to_broadcast([P, 4, HALF]),
-                        in1=ps3[:, :, (1 - half) * HALF : (2 - half) * HALF],
+                        out=o, in0=tab.unsqueeze(1).to_broadcast([P, 4, 2, HALF]),
+                        in1=ps3[:, :, d0 : d0 + HALF].unsqueeze(2).to_broadcast([P, 4, 2, HALF]),
                         op=ALU.mult,
                     )
             if bi == nb - 1:

from contextlib import ExitStack
import math

import concourse.mybir as mybir

F32 = mybir.dt.float32
BF16 = mybir.dt.bfloat16
I32 = mybir.dt.int32
U32 = mybir.dt.uint32
U8 = mybir.dt.uint8
FP4 = mybir.dt.float4_e2m1fn_x4
ALU = mybir.AluOpType
ACT = mybir.ActivationFunctionType

NB, T, C = 2, 1536, 2048
NH, NKV, HS = 16, 4, 128
HALF = HS // 2
EPS = 1e-6
THETA = 10000.0
P = 128
PASSES = C // 512
NJ = T // P
NT = NB * NJ
BANK = 512
FLOPS = 2 * NB * T * C * (NH * HS + 2 * NKV * HS)

JCH = ((0, 3), (3, 7), (7, 12))
TCH = ((0, 6), (6, 12))
J1 = 3
W_ORDER1 = (5, 0, 1, 2, 3, 4)
GSZ = 3
LAST_SPLIT = (2, 1)
FUSED = (2, 3, 4)
V_TAIL = 7
N_LATE = 0
LAG_SS = 1
LAG_V = 2
LAG_RS = {1: 3, 2: 5, 3: 7}
N_WARM = 15
T1_BUFS = 8
T2_BUFS = 5
TAB_PLAN = (((6, 12),), {}, ((0, 6),))
LOAD_PLAN = {1: ((3,),), 6: ((4,),), 11: ((5,),), 16: ((0, 1),), 21: ((1, 1),), 50: ((0, 2),), 56: ((1, 2),)}


def tile_attention_pa_kernel(
    tc, x_words, x_scales, Wq_words, Wq_scales, Wkv_words, Wkv_scales,
    q_scale, k_scale, v1, value_lambda, out_0, out_1, out_2,
):
    nc = tc.nc
    out0f = out_0.rearrange("b t h d -> (b t) (h d)")
    out1f = out_1.rearrange("b t h d -> (b t) (h d)")
    out2f = out_2.rearrange("b t h d -> (b t) (h d)")
    v1f = v1.rearrange("b t h d -> (b t) (h d)")

    with ExitStack() as ctx:
        ctx.enter_context(tc.manual_schedule())
        keep = ctx.enter_context(tc.tile_pool(name="keep", bufs=1))
        psum = ctx.enter_context(tc.psum_pool(name="psum", bufs=8))
        work = ctx.enter_context(tc.tile_pool(name="work", bufs=2))

        chunks = [(b, c) for c in range(len(JCH)) for b in range(NB)]
        xc, xs, v1c = {}, {}, {}
        for b, c in chunks:
            nj = JCH[c][1] - JCH[c][0]
            xc[(b, c)] = keep.tile([P, PASSES, 256 * nj], U8, name="xc%d%d" % (b, c), align_bytes=64)
            xs[(b, c)] = keep.tile([P, PASSES, P * nj], U8, name="xs%d%d" % (b, c), align_bytes=64)
            v1c[(b, c)] = keep.tile([P, nj, BANK], BF16, name="v1c%d%d" % (b, c))
        wc = [keep.tile([P, PASSES, 2 * BANK], U8, name="wc%d" % w, align_bytes=64) for w in range(6)]
        ws = [keep.tile([P, PASSES, BANK], U8, name="ws%d" % w, align_bytes=64) for w in range(6)]

        ones = keep.tile([P, 8], F32, name="ones")
        a8 = keep.tile([P, 8], F32, name="a8")
        b8 = keep.tile([P, 8], F32, name="b8")
        turn = keep.tile([P, HALF], F32, name="turn")
        pos = keep.tile([P, NJ], F32, name="pos")
        yt = keep.tile([P, NJ, HALF], F32, name="yt")
        ki = keep.tile([P, NJ, HALF], U32, name="ki")
        kf = keep.tile([P, NJ, HALF], F32, name="kf")
        ang = keep.tile([P, NJ, 3, HALF], F32, name="ang")
        t_lo = keep.tile([P, NJ, 2, HS], F32, name="t_lo")
        t_hi = keep.tile([P, NJ, 2, HS], F32, name="t_hi")
        gw = keep.tile([P, 2, HS], BF16, name="gw")
        w_lo = keep.tile([P, 2, 2, HALF], BF16, name="w_lo")
        w_hi = keep.tile([P, 2, 2, HALF], BF16, name="w_hi")
        lam = keep.tile([P, 1], BF16, name="lam")
        cl = keep.tile([P, 1], F32, name="cl")
        eps_t = keep.tile([P, 1], F32, name="eps_t")
        junk = keep.tile([P, 8, HS], BF16, name="junk")
        wz = keep.tile([P, BANK], BF16, name="wz")

        def zero_plane(t):
            nc.vector.memset(t[:].rearrange("p g n -> p (g n)").bitcast(I32), 0)

        def load_codes(t, src):
            nc.sync.dma_start(out=t[:].bitcast(I32), in_=src.rearrange("g p n -> p g n").bitcast(I32))

        def load_scales(t, src):
            for q in range(4):
                nc.sync.dma_start(
                    out=t[32 * q : 32 * q + 4, :, :].bitcast(I32),
                    in_=src[:, 4 * q : 4 * q + 4, :].rearrange("g r n -> r g n").bitcast(I32),
                )

        def x_cols(b, c, width):
            return slice(width * (NJ * b + JCH[c][0]), width * (NJ * b + JCH[c][1]))

        def load_x_codes(b, c):
            load_codes(xc[(b, c)], x_words[:, :, x_cols(b, c, 256)])

        def load_x_scales(b, c):
            load_scales(xs[(b, c)], x_scales[:, :, x_cols(b, c, P)])

        def load_v1(b, c):
            nc.sync.dma_start(
                out=v1c[(b, c)][:],
                in_=v1f[x_cols(b, c, P), :].rearrange("(n p) d -> p n d", p=P),
            )

        def load_w_codes(w):
            if w < 4:
                load_codes(wc[w], Wq_words[:, :, 2 * BANK * w : 2 * BANK * (w + 1)])
            else:
                load_codes(wc[w], Wkv_words[:, :, 2 * BANK * (w - 4) : 2 * BANK * (w - 3)])

        def load_w_scales(w):
            if w < 4:
                load_scales(ws[w], Wq_scales[:, :, BANK * w : BANK * (w + 1)])
            else:
                load_scales(ws[w], Wkv_scales[:, :, BANK * (w - 4) : BANK * (w - 3)])

        w_first = W_ORDER1[0]
        nc.gpsimd.memset(wz[:], 0.0)
        nc.gpsimd.iota(pos[:], pattern=[[P, NJ]], base=0, channel_multiplier=1, allow_small_or_imprecise_dtypes=True)
        nc.gpsimd.dma_start(out=gw[:, 0, :], in_=q_scale.partition_broadcast(P))
        nc.gpsimd.dma_start(out=gw[:, 1, :], in_=k_scale.partition_broadcast(P))
        nc.gpsimd.dma_start(out=lam[:], in_=value_lambda.partition_broadcast(P))

        nc.vector.memset(ones[:], 1.0)
        zero_plane(xs[(0, 0)])
        zero_plane(ws[w_first])
        load_w_codes(w_first)
        load_x_codes(0, 0)
        load_x_scales(0, 0)
        load_w_scales(w_first)

        nc.scalar.activation(out=junk[:, 0, 0:1], in_=ones[:, 0:1], func=ACT.Sin)

        warm = psum.tile([P, BANK], F32, name="acc", tag="acc")
        for i in range(N_WARM):
            nc.tensor.matmul(out=warm[:], lhsT=wz[:, 0:P], rhs=wz[:], start=True, stop=True)

        for m in range(8):
            nc.scalar.mul(out=a8[:, m : m + 1], in_=ones[:, m : m + 1], mul=THETA ** (-8.0 * m / HALF) / (2.0 * math.pi))
            nc.scalar.mul(out=b8[:, m : m + 1], in_=ones[:, m : m + 1], mul=THETA ** (-1.0 * m / HALF))
        zero_plane(xs[(1, 0)])
        load_x_codes(1, 0)
        load_x_scales(1, 0)
        load_v1(0, 0)
        load_v1(1, 0)
        nc.vector.memset(eps_t[:], EPS)
        nc.vector.tensor_tensor(
            out=turn[:].rearrange("p (m n) -> p m n", n=8),
            in0=a8[:].unsqueeze(2).to_broadcast([P, 8, 8]),
            in1=b8[:].unsqueeze(1).to_broadcast([P, 8, 8]),
            op=ALU.mult,
        )

        def tab_scalar_1(j0, j1):
            for j in range(j0, j1):
                nc.scalar.activation(out=yt[:, j, :], in_=turn[:], func=ACT.Copy, scale=pos[:, j : j + 1])
            nc.scalar.activation(out=ki[:, j0:j1, :], in_=yt[:, j0:j1, :], func=ACT.Copy)
            nc.scalar.activation(out=kf[:, j0:j1, :], in_=ki[:, j0:j1, :], func=ACT.Copy)

        def tab_vector(j0, j1):
            y = yt[:, j0:j1, :]
            e = ang[:, j0:j1, 0, :]
            nc.vector.tensor_tensor(out=y, in0=y, in1=kf[:, j0:j1, :], op=ALU.subtract)
            nc.vector.scalar_tensor_tensor(out=e, in0=y, scalar=0.5, in1=y, op0=ALU.is_gt, op1=ALU.subtract)


        def tab_scalar_2(j0, j1):
            e = ang[:, j0:j1, 0, :]
            nc.scalar.activation(out=kf[:, j0:j1, :], in_=e, func=ACT.Abs)
            nc.scalar.activation(out=ang[:, j0:j1, 1, :], in_=kf[:, j0:j1, :], func=ACT.Copy, scale=-1.0, bias=0.25)
            nc.scalar.mul(out=ang[:, j0:j1, 2, :], in_=e, mul=-1.0)
            a = ang[:, j0:j1, :, :].rearrange("p j x i -> p (j x i)")
            nc.scalar.activation(out=a, in_=a, func=ACT.Sin, scale=2.0 * math.pi)

        def tab_products(j0, j1, eng=nc.gpsimd):
            nj = j1 - j0
            for tab, first, gain in ((t_lo, 1, w_lo), (t_hi, 0, w_hi)):
                eng.tensor_tensor(
                    out=tab[:, j0:j1, :, :],
                    in0=ang[:, j0:j1, first : first + 2, :].rearrange("p j x i -> p j (x i)").unsqueeze(2).to_broadcast([P, nj, 2, HS]),
                    in1=gain[:].rearrange("p k x i -> p k (x i)").unsqueeze(1).to_broadcast([P, nj, 2, HS]),
                    op=ALU.mult,
                )

        nc.gpsimd.tensor_copy(out=w_lo[:], in_=gw[:, :, 0:HALF].unsqueeze(2).to_broadcast([P, 2, 2, HALF]))
        nc.gpsimd.tensor_copy(out=w_hi[:], in_=gw[:, :, HALF:HS].unsqueeze(2).to_broadcast([P, 2, 2, HALF]))

        def load_w(w):
            load_w_codes(w)
            load_w_scales(w)

        def load_x(b, c):
            load_x_codes(b, c)
            load_x_scales(b, c)
            load_v1(b, c)

        tab_scalar_1(*TCH[0])
        for w in W_ORDER1[1:4]:
            zero_plane(ws[w])
        load_w(W_ORDER1[1])
        tab_vector(*TCH[0])
        tab_scalar_1(*TCH[1])
        tab_scalar_2(*TCH[0])
        for w in W_ORDER1[4:]:
            zero_plane(ws[w])
        for c in range(1, len(JCH)):
            for b in range(NB):
                zero_plane(xs[(b, c)])
        load_w(W_ORDER1[2])
        tab_vector(*TCH[1])
        tab_scalar_2(*TCH[1])
        nc.scalar.activation(out=junk[:, 0, 0:1], in_=ones[:, 0:1], func=ACT.Abs_reciprocal_sqrt)
        nc.vector.tensor_scalar(out=cl[:], in0=lam[:], scalar1=-1.0, scalar2=1.0, op0=ALU.mult, op1=ALU.add)
        for j0, j1 in TAB_PLAN[2]:
            tab_products(j0, j1, nc.vector)
        for j0, j1 in TAB_PLAN[0]:
            tab_products(j0, j1)

        jobs = []
        for w in W_ORDER1:
            for b in range(NB):
                for j in range(J1):
                    jobs.append((j, b, w))
        rest = [(j, b) for j in range(J1, NJ) for b in range(NB)]
        for i in range(len(rest)):
            for w in range(5):
                jobs.append(rest[i] + (w,))
            if i < len(rest) - V_TAIL:
                jobs.append(rest[i] + (5,))
        for i in range(len(rest) - V_TAIL, len(rest)):
            jobs.append(rest[i] + (5,))
        n_jobs = len(jobs)
        late = rest[len(rest) - N_LATE :] if N_LATE else []
        fused_job = [(w in FUSED or (j, b) in late) and w != 5 for j, b, w in jobs]

        qk = [n for n in range(n_jobs) if jobs[n][2] != 5]
        sizes = [GSZ] * ((len(qk) - sum(LAST_SPLIT)) // GSZ) + list(LAST_SPLIT)
        assert sum(sizes) == len(qk)
        groups = []
        place = {}
        for size in sizes:
            first = sum(len(g) for g in groups)
            groups.append(qk[first : first + size])
            for i in range(size):
                place[qk[first + i]] = (len(groups) - 1, i)

        def chunk_of(j):
            c = [i for i in range(len(JCH)) if JCH[i][0] <= j < JCH[i][1]][0]
            return c, j - JCH[c][0]

        acc = {}
        t1 = {}
        t2 = {}
        ssq = {}
        rinv = {}
        rs_queue = []
        rs_done = [0]

        def emit_pe(n):
            j, b, w = jobs[n]
            c, l = chunk_of(j)
            ps = psum.tile([P, BANK], F32, name="acc", tag="acc")
            acc[n] = ps
            for g in range(PASSES):
                nc.tensor.matmul_mx(
                    out=ps[:],
                    lhsT=xc[(b, c)][:, g, 256 * l : 256 * (l + 1)].bitcast(FP4),
                    lhsT_scale=xs[(b, c)][:, g, P * l : P * (l + 1)],
                    rhs=wc[w][:, g, :].bitcast(FP4),
                    rhs_scale=ws[w][:, g, :],
                    start=(g == 0),
                    stop=(g == PASSES - 1),
                )

        def emit_ss(n):
            j, b, w = jobs[n]
            if w == 5:
                return
            gi, bi = place[n]
            grp = groups[gi]
            if bi == 0:
                ssq[gi] = work.tile([P, 4 * GSZ], F32, name="ss", tag="ss", bufs=6)
                rinv[gi] = work.tile([P, 4 * GSZ], F32, name="ri", tag="ri", bufs=10)
            ps = acc[n]
            for h in range(4):
                nc.scalar.activation(
                    out=junk[:, 4 * (n % 2) + h, :], in_=ps[:, h * HS : (h + 1) * HS], func=ACT.Square,
                    accum_out=ssq[gi][:, 4 * bi + h : 4 * bi + h + 1],
                )
            b0 = bi
            if not fused_job[n]:
                if bi + 1 < len(grp) and not fused_job[grp[bi + 1]]:
                    return
                while b0 > 0 and not fused_job[grp[b0 - 1]]:
                    b0 -= 1
            nc.scalar.activation(
                out=rinv[gi][:, 4 * b0 : 4 * bi + 4], in_=ssq[gi][:, 4 * b0 : 4 * bi + 4], func=ACT.Abs_reciprocal_sqrt,
                scale=1.0 / HS, bias=eps_t[:, 0:1],
            )

        def store_banks(gi, banks):
            t = t1[gi]
            i = 0
            while i < len(banks):
                j, b, w = jobs[groups[gi][banks[i]]]
                k = i
                while (
                    k + 1 < len(banks) and banks[k + 1] == banks[k] + 1 and w + k + 1 - i < 4
                    and jobs[groups[gi][banks[k + 1]]] == (j, b, w + k + 1 - i)
                ):
                    k += 1
                tok = P * (NJ * b + j)
                src = t[:, banks[i] * BANK : (banks[k] + 1) * BANK]
                if w < 4:
                    nc.sync.dma_start(out=out0f[tok : tok + P, w * BANK : (w + k + 1 - i) * BANK], in_=src)
                else:
                    nc.sync.dma_start(out=out1f[tok : tok + P, :], in_=src)
                i = k + 1

        def emit_v(n, step):
            j, b, w = jobs[n]
            c, l = chunk_of(j)
            tok = P * (NJ * b + j)
            ps = acc[n]
            if w == 5:
                vo = work.tile([P, BANK], F32, name="vo", tag="vo", bufs=6)
                nc.vector.scalar_tensor_tensor(
                    out=vo[:], in0=v1c[(b, c)][:, l, :], scalar=cl[:, 0:1], in1=ps[:], op0=ALU.mult, op1=ALU.add
                )
                nc.sync.dma_start(out=out2f[tok : tok + P, :], in_=vo[:])
                return
            gi, bi = place[n]
            grp = groups[gi]
            nb = len(grp)
            if bi == 0:
                t1[gi] = work.tile([P, nb * BANK], F32, name="t1", tag="t1", bufs=T1_BUFS)
                t2[gi] = work.tile([P, nb * BANK], F32, name="t2", tag="t2", bufs=T2_BUFS)
            kind = 0 if w < 4 else 1
            ps3 = ps[:].rearrange("p (h d) -> p h d", h=4)
            parts = (
                (t1[gi], t_lo[:, j, kind, :].rearrange("p (x i) -> p x i", x=2), 0),
                (t2[gi], t_hi[:, j, kind, :].rearrange("p (x i) -> p x i", x=2), HALF),
            )
            for dst, tab, d0 in parts:
                o = dst[:, bi * BANK : (bi + 1) * BANK].rearrange("p (h x i) -> p h x i", h=4, x=2)
                if fused_job[n]:
                    for h in range(4):
                        nc.vector.scalar_tensor_tensor(
                            out=o[:, h, :, :], in0=tab, scalar=rinv[gi][:, 4 * bi + h : 4 * bi + h + 1],
                            in1=ps3[:, h, d0 : d0 + HALF].unsqueeze(1).to_broadcast([P, 2, HALF]),
                            op0=ALU.mult, op1=ALU.mult,
                        )
                else:
                    nc.vector.tensor_tensor(
                        out=o, in0=tab.unsqueeze(1).to_broadcast([P, 4, 2, HALF]),
                        in1=ps3[:, :, d0 : d0 + HALF].unsqueeze(2).to_broadcast([P, 4, 2, HALF]),
                        op=ALU.mult,
                    )
            if bi == nb - 1:
                nc.gpsimd.tensor_tensor(out=t1[gi][:], in0=t1[gi][:], in1=t2[gi][:], op=ALU.add)
                lag = LAG_RS[nb]
                rs_queue.append((step + lag, gi, -1))
                k = 0
                for i in range(nb):
                    if not fused_job[grp[i]]:
                        rs_queue.append((step + lag + k, gi, i))
                        k += 1
                rs_queue.append((step + lag + max(0, k - 1), gi, -2))

        def emit_rs(gi, i):
            grp = groups[gi]
            t = t1[gi]
            if i == -1:
                store_banks(gi, [k for k in range(len(grp)) if fused_job[grp[k]]])
            elif i == -2:
                store_banks(gi, [k for k in range(len(grp)) if not fused_job[grp[k]]])
            else:
                for h in range(4 * i, 4 * i + 4):
                    nc.scalar.activation(
                        out=t[:, h * HS : (h + 1) * HS], in_=t[:, h * HS : (h + 1) * HS], func=ACT.Copy,
                        scale=rinv[gi][:, h : h + 1],
                    )

        step = 0
        while step < n_jobs + LAG_V or rs_done[0] < len(rs_queue):
            for what in LOAD_PLAN.get(step, ()):
                if len(what) == 1:
                    load_w(W_ORDER1[what[0]])
                else:
                    load_x(*what)
            if step < n_jobs:
                emit_pe(step)
            if 0 <= step - LAG_SS < n_jobs:
                emit_ss(step - LAG_SS)
            while rs_done[0] < len(rs_queue) and rs_queue[rs_done[0]][0] <= step:
                emit_rs(*rs_queue[rs_done[0]][1:])
                rs_done[0] += 1
            if 0 <= step - LAG_V < n_jobs:
                emit_v(step - LAG_V, step)
            for j0, j1 in TAB_PLAN[1].get(step, ()):
                tab_products(j0, j1)
            step += 1
